import numpy as np
import ml_dtypes


def mxq(x, axis, fmt="e4m3"):
    dtype, down = {"e4m3": (ml_dtypes.float8_e4m3fn, 7), "e5m2": (ml_dtypes.float8_e5m2, 14)}[fmt]
    v = np.moveaxis(np.asarray(x, np.float32).astype(ml_dtypes.bfloat16).astype(np.float64), axis, -1)
    blocks = v.reshape(v.shape[:-1] + (-1, 32))
    amax = np.abs(blocks).max(-1, keepdims=True)
    byte = np.maximum(np.where(amax > 0, np.frexp(amax)[1] - 1 + 127, 0) - down, 1)
    scale = np.exp2(byte - 127.0)
    codes = (blocks / scale).astype(np.float32).astype(dtype).astype(np.float64)
    return np.moveaxis((codes * scale).reshape(v.shape), -1, axis)


WIDE = False


def mx_kscale(k):
    if not WIDE:
        return np.ones(k)
    levels = np.array([10, -10, 5, -5, 0])
    a = np.random.permutation(np.resize(levels, k // 512 * 4)).reshape(k // 512, 4)
    idx = np.arange(k)
    return np.exp2(a[idx // 512, idx % 128 // 32])


BF16 = ml_dtypes.bfloat16


def bf(x):
    return np.asarray(x, np.float32).astype(BF16)


def f64(x):
    return np.asarray(x).astype(np.float64)


B, L0, L1, L2, L3 = 1024, 1024, 512, 512, 512
DT = 1.0
TAU_J = 10.0
TAU_M = 20.0
KAPPA_J = 0.25
THRESH = 0.4
X_DECAY = 20.0
P_FIRE = 0.2


def lif_update(j, v, x, total_input):
    j = j + (DT / TAU_J) * (-KAPPA_J * j + total_input)
    v = v + (DT / TAU_M) * (-v + j)
    spikes = np.where(v > THRESH, 1.0, 0.0)
    v = v * (1.0 - spikes)
    x = x + (-x / X_DECAY + spikes)
    return j, v, spikes, x


def setup_inputs():
    s, t = mx_kscale(L1), mx_kscale(L3)
    return {
        "e_gen2": bf(np.random.random((B, L2)) * 2.0 + np.random.standard_normal((B, L2)) * 0.7),
        "e_disc2": bf(np.random.random((B, L2)) * 2.0 + np.random.standard_normal((B, L2)) * 0.7),
        "e_gen1": bf((np.random.random((B, L1)) * 2.0 + np.random.standard_normal((B, L1)) * 0.7) * s),
        "e_disc3": bf(((np.random.random((B, L3)) < P_FIRE) + np.random.standard_normal((B, L3)) * 0.7) * t),
        "j2": bf(np.random.standard_normal((B, L2)) * 1.5),
        "v2": bf(np.random.standard_normal((B, L2)) * 0.4),
        "x2": bf(np.random.random((B, L2)) * 2.0),
        "Eg1": bf(np.random.standard_normal((L2, L1)) * 2.0 / np.sqrt(L1) / s),
        "Ed2": bf(np.random.standard_normal((L2, L3)) * 2.0 / np.sqrt(L3) / t),
    }


def reference(e_gen2, e_disc2, e_gen1, e_disc3, j2, v2, x2, Eg1, Ed2):
    total2 = (-(f64(e_gen2) + f64(e_disc2))
              + (mxq(f64(e_gen1), 1, "e4m3") @ mxq(f64(Eg1), 1, "e4m3").T)
              + (mxq(f64(e_disc3), 1, "e4m3") @ mxq(f64(Ed2), 1, "e4m3").T))
    j2n, v2n, s2n, x2n = lif_update(f64(j2), f64(v2), f64(x2), total2)
    return np.concatenate([j2n, v2n, x2n, s2n], axis=-1)

@@ -1,0 +1,202 @@
+from contextlib import ExitStack
+
+import concourse.mybir as mybir
+from concourse.masks import make_identity
+
+F32 = mybir.dt.float32
+BF16 = mybir.dt.bfloat16
+U32 = mybir.dt.uint32
+U8 = mybir.dt.uint8
+FP8X4 = mybir.dt.float8_e4m3fn_x4
+ALU = mybir.AluOpType
+
+P = 128
+BATCH = 1024
+NEURONS = 512
+K = 512
+TILES = BATCH // P
+PAIRS = TILES // 2
+PACK = 4
+WORDS = K // 2
+HALVES = WORDS // P
+W_BLOCKS = NEURONS // P
+
+FLOPS = 2 * 2 * BATCH * NEURONS * K
+
+DT = 1.0
+TAU_J = 10.0
+TAU_M = 20.0
+KAPPA_J = 0.25
+THRESH = 0.4
+X_DECAY = 20.0
+J_GAIN = DT / TAU_J
+J_KEEP = 1.0 - J_GAIN * KAPPA_J
+V_GAIN = DT / TAU_M
+V_KEEP = 1.0 - V_GAIN
+X_KEEP = 1.0 - 1.0 / X_DECAY
+
+J_COLS = slice(0, NEURONS)
+V_COLS = slice(NEURONS, 2 * NEURONS)
+X_COLS = slice(2 * NEURONS, 3 * NEURONS)
+S_COLS = slice(3 * NEURONS, 4 * NEURONS)
+
+
+def by_tile(dram):
+    return dram.rearrange("(p t) c -> p t c", t=TILES)
+
+
+def k_onto_partitions(nc, banks, ident, block_a, block_b, grouped_words, copy):
+    turned = banks.tile([P, 2, HALVES, P], F32, name="turned")
+    for i, block in enumerate((block_a, block_b)):
+        for u in range(HALVES):
+            nc.tensor.transpose(turned[:, i, u, :], block[:, u * P : (u + 1) * P], ident[:])
+    copy(out=grouped_words, in_=turned[:].rearrange("p i u r -> p i r u"))
+
+
+def tile_bspncn_pb_kernel(
+    tc, e_gen2, e_disc2, e_gen1, e_disc3, j2, v2, x2, Eg1, Ed2, out
+):
+    nc = tc.nc
+    with ExitStack() as ctx:
+        ctx.enter_context(tc.manual_schedule())
+        const = ctx.enter_context(tc.tile_pool(name="const", bufs=1))
+        inputs = ctx.enter_context(tc.tile_pool(name="inputs", bufs=PAIRS))
+        work = ctx.enter_context(tc.tile_pool(name="work", bufs=2))
+        results = ctx.enter_context(tc.tile_pool(name="results", bufs=TILES))
+        banks = ctx.enter_context(tc.psum_pool(name="banks", bufs=4))
+        sums = ctx.enter_context(tc.psum_pool(name="sums", bufs=4))
+
+        ident = const.tile([P, P], F32, name="ident")
+        make_identity(nc, ident[:])
+
+        w_raw = []
+        for o, w in enumerate((Eg1, Ed2)):
+            raw = const.tile([P, W_BLOCKS, K], BF16, name="w_raw%d" % o)
+            nc.sync.dma_start(out=raw[:], in_=w.rearrange("(r p) k -> p r k", p=P))
+            w_raw.append(raw)
+        sources = (
+            ("e_gen1", e_gen1),
+            ("e_disc3", e_disc3),
+            ("e_gen2", e_gen2),
+            ("e_disc2", e_disc2),
+            ("j2", j2),
+            ("v2", v2),
+            ("x2", x2),
+        )
+        loaded = []
+        for pair in range(PAIRS):
+            tiles = {}
+            for name, dram in sources:
+                tiles[name] = inputs.tile([P, 2, NEURONS], BF16, name=name)
+                nc.sync.dma_start(
+                    out=tiles[name][:], in_=by_tile(dram)[:, 2 * pair : 2 * pair + 2, :]
+                )
+            loaded.append(tiles)
+
+        w_grouped = const.tile([P, 2, W_BLOCKS, P, PACK], BF16, name="w_grouped", align_bytes=64)
+        w_codes = const.tile([P, 2, NEURONS], U32, name="w_codes", align_bytes=64)
+        w_scales = const.tile([P, 2, NEURONS], U8, name="w_scales", align_bytes=64)
+        for o in range(2):
+            raw_words = w_raw[o][:].bitcast(F32)
+            grouped_words = w_grouped[:].bitcast(F32)
+            k_onto_partitions(
+                nc, banks, ident, raw_words[:, 0, :], raw_words[:, 1, :],
+                grouped_words[:, o, 0:2], nc.vector.tensor_copy,
+            )
+            k_onto_partitions(
+                nc, banks, ident, raw_words[:, 2, :], raw_words[:, 3, :],
+                grouped_words[:, o, 2:4], nc.scalar.copy,
+            )
+            nc.vector.quantize_mx(
+                out=w_codes[:, o, :].bitcast(FP8X4),
+                scales=w_scales[:, o, :],
+                in_=w_grouped[:, o].rearrange("p r c j -> p (r c j)"),
+            )
+
+        for pair in range(PAIRS):
+            got = loaded[pair]
+
+            grouped = work.tile([P, 2, 2, P, PACK], BF16, name="grouped", align_bytes=64)
+            codes = work.tile([P, 2, 2, P], U32, name="codes", align_bytes=64)
+            scales = work.tile([P, 2, 2, P], U8, name="scales", align_bytes=64)
+            for a in range(2):
+                k_onto_partitions(
+                    nc, banks, ident,
+                    got["e_gen1"][:].bitcast(F32)[:, a, :],
+                    got["e_disc3"][:].bitcast(F32)[:, a, :],
+                    grouped[:].bitcast(F32)[:, a], nc.scalar.copy,
+                )
+            nc.vector.quantize_mx(
+                out=codes[:].rearrange("p a o r -> p (a o r)").bitcast(FP8X4),
+                scales=scales[:].rearrange("p a o r -> p (a o r)"),
+                in_=grouped[:].rearrange("p a o r j -> p (a o r j)"),
+            )
+
+            j_kept = work.tile([P, 2, NEURONS], F32, name="j_kept")
+            nc.scalar.mul(out=j_kept[:], in_=got["j2"][:], mul=J_KEEP)
+            v_kept = work.tile([P, 2, NEURONS], F32, name="v_kept")
+            nc.scalar.mul(out=v_kept[:], in_=got["v2"][:], mul=V_KEEP)
+            own_err = work.tile([P, 2, NEURONS], F32, name="own_err")
+            for a in range(2):
+                nc.vector.tensor_tensor(
+                    out=own_err[:, a, :], in0=got["e_gen2"][:, a, :],
+                    in1=got["e_disc2"][:, a, :], op=ALU.add,
+                )
+            rest = work.tile([P, 2, NEURONS], F32, name="rest")
+            for a in range(2):
+                nc.vector.scalar_tensor_tensor(
+                    out=rest[:, a, :], in0=own_err[:, a, :], scalar=-J_GAIN,
+                    in1=j_kept[:, a, :], op0=ALU.mult, op1=ALU.add,
+                )
+
+            fed_back = []
+            for a in range(2):
+                acc = sums.tile([P, NEURONS], F32, name="acc")
+                for o in range(2):
+                    nc.tensor.matmul_mx(
+                        out=acc[:],
+                        lhsT=codes[:, a, o, :].bitcast(FP8X4),
+                        lhsT_scale=scales[:, a, o, :],
+                        rhs=w_codes[:, o, :].bitcast(FP8X4),
+                        rhs_scale=w_scales[:, o, :],
+                        start=(o == 0),
+                        stop=(o == 1),
+                    )
+                fed_back.append(acc)
+
+            res = [results.tile([P, 4 * NEURONS], F32, name="res") for a in range(2)]
+            v_pre = work.tile([P, 2, NEURONS], F32, name="v_pre")
+            for a in range(2):
+                nc.vector.scalar_tensor_tensor(
+                    out=res[a][:, J_COLS], in0=fed_back[a][:], scalar=J_GAIN,
+                    in1=rest[:, a, :], op0=ALU.mult, op1=ALU.add,
+                )
+            for a in range(2):
+                nc.vector.scalar_tensor_tensor(
+                    out=v_pre[:, a, :], in0=res[a][:, J_COLS], scalar=V_GAIN,
+                    in1=v_kept[:, a, :], op0=ALU.mult, op1=ALU.add,
+                )
+            for a in range(2):
+                nc.vector.scalar_tensor_tensor(
+                    out=res[a][:, V_COLS], in0=v_pre[:, a, :], scalar=THRESH,
+                    in1=v_pre[:, a, :], op0=ALU.is_le, op1=ALU.mult,
+                )
+            for a in range(2):
+                nc.sync.dma_start(
+                    out=by_tile(out)[:, 2 * pair + a, 0 : 2 * NEURONS],
+                    in_=res[a][:, 0 : 2 * NEURONS],
+                )
+            for a in range(2):
+                nc.vector.tensor_single_scalar(
+                    out=res[a][:, S_COLS], in_=v_pre[:, a, :], scalar=THRESH, op=ALU.is_gt
+                )
+            for a in range(2):
+                nc.vector.scalar_tensor_tensor(
+                    out=res[a][:, X_COLS], in0=got["x2"][:, a, :], scalar=X_KEEP,
+                    in1=res[a][:, S_COLS], op0=ALU.mult, op1=ALU.add,
+                )
+            for a in range(2):
+                nc.sync.dma_start(
+                    out=by_tile(out)[:, 2 * pair + a, 2 * NEURONS : 4 * NEURONS],
+                    in_=res[a][:, 2 * NEURONS : 4 * NEURONS],
+                )

@@ -45,12 +45,12 @@ def by_tile(dram):
     return dram.rearrange("(p t) c -> p t c", t=TILES)
 
 
-def k_onto_partitions(nc, banks, ident, block_a, block_b, grouped_words, copy):
+def k_onto_partitions(nc, banks, ident, block_a, block_b, grouped_words):
     turned = banks.tile([P, 2, HALVES, P], F32, name="turned")
     for i, block in enumerate((block_a, block_b)):
         for u in range(HALVES):
             nc.tensor.transpose(turned[:, i, u, :], block[:, u * P : (u + 1) * P], ident[:])
-    copy(out=grouped_words, in_=turned[:].rearrange("p i u r -> p i r u"))
+    nc.scalar.copy(out=grouped_words, in_=turned[:].rearrange("p i u r -> p i r u"))
 
 
 def tile_bspncn_pb_kernel(
@@ -69,85 +69,88 @@ def tile_bspncn_pb_kernel(
         ident = const.tile([P, P], F32, name="ident")
         make_identity(nc, ident[:])
 
+        sources = {
+            "e_gen2": e_gen2, "e_disc2": e_disc2, "e_gen1": e_gen1, "e_disc3": e_disc3,
+            "j2": j2, "v2": v2, "x2": x2,
+        }
+        loaded = {}
+
+        def load(names, pair):
+            for name in names:
+                sbuf = inputs.tile([P, 2, NEURONS], BF16, name=name)
+                nc.sync.dma_start(
+                    out=sbuf[:], in_=by_tile(sources[name])[:, 2 * pair : 2 * pair + 2, :]
+                )
+                loaded[(name, pair)] = sbuf
+
+        for pair in range(PAIRS):
+            load(("j2", "e_gen2", "e_disc2"), pair)
         w_raw = []
         for o, w in enumerate((Eg1, Ed2)):
             raw = const.tile([P, W_BLOCKS, K], BF16, name="w_raw%d" % o)
             nc.sync.dma_start(out=raw[:], in_=w.rearrange("(r p) k -> p r k", p=P))
             w_raw.append(raw)
-        sources = (
-            ("e_gen1", e_gen1),
-            ("e_disc3", e_disc3),
-            ("e_gen2", e_gen2),
-            ("e_disc2", e_disc2),
-            ("j2", j2),
-            ("v2", v2),
-            ("x2", x2),
-        )
-        loaded = []
+        load(("e_gen1", "e_disc3"), 0)
         for pair in range(PAIRS):
-            tiles = {}
-            for name, dram in sources:
-                tiles[name] = inputs.tile([P, 2, NEURONS], BF16, name=name)
-                nc.sync.dma_start(
-                    out=tiles[name][:], in_=by_tile(dram)[:, 2 * pair : 2 * pair + 2, :]
+            if pair + 1 < PAIRS:
+                load(("e_gen1", "e_disc3"), pair + 1)
+            load(("v2", "x2"), pair)
+
+        rest = []
+        for pair in range(PAIRS):
+            j_kept = work.tile([P, 2, NEURONS], F32, name="j_kept")
+            nc.scalar.mul(out=j_kept[:], in_=loaded[("j2", pair)][:], mul=J_KEEP)
+            own_err = work.tile([P, 2, NEURONS], F32, name="own_err")
+            for a in range(2):
+                nc.vector.tensor_tensor(
+                    out=own_err[:, a, :], in0=loaded[("e_gen2", pair)][:, a, :],
+                    in1=loaded[("e_disc2", pair)][:, a, :], op=ALU.add,
                 )
-            loaded.append(tiles)
+            rest.append(inputs.tile([P, 2, NEURONS], F32, name="rest"))
+            for a in range(2):
+                nc.vector.scalar_tensor_tensor(
+                    out=rest[pair][:, a, :], in0=own_err[:, a, :], scalar=-J_GAIN,
+                    in1=j_kept[:, a, :], op0=ALU.mult, op1=ALU.add,
+                )
 
         w_grouped = const.tile([P, 2, W_BLOCKS, P, PACK], BF16, name="w_grouped", align_bytes=64)
         w_codes = const.tile([P, 2, NEURONS], U32, name="w_codes", align_bytes=64)
         w_scales = const.tile([P, 2, NEURONS], U8, name="w_scales", align_bytes=64)
         for o in range(2):
             raw_words = w_raw[o][:].bitcast(F32)
-            grouped_words = w_grouped[:].bitcast(F32)
-            k_onto_partitions(
-                nc, banks, ident, raw_words[:, 0, :], raw_words[:, 1, :],
-                grouped_words[:, o, 0:2], nc.vector.tensor_copy,
-            )
-            k_onto_partitions(
-                nc, banks, ident, raw_words[:, 2, :], raw_words[:, 3, :],
-                grouped_words[:, o, 2:4], nc.scalar.copy,
-            )
+            for r in range(0, W_BLOCKS, 2):
+                k_onto_partitions(
+                    nc, banks, ident, raw_words[:, r, :], raw_words[:, r + 1, :],
+                    w_grouped[:].bitcast(F32)[:, o, r : r + 2],
+                )
+        for o in range(2):
             nc.vector.quantize_mx(
                 out=w_codes[:, o, :].bitcast(FP8X4),
                 scales=w_scales[:, o, :],
                 in_=w_grouped[:, o].rearrange("p r c j -> p (r c j)"),
             )
 
-        for pair in range(PAIRS):
-            got = loaded[pair]
-
+        def quantise_streams(pair):
             grouped = work.tile([P, 2, 2, P, PACK], BF16, name="grouped", align_bytes=64)
             codes = work.tile([P, 2, 2, P], U32, name="codes", align_bytes=64)
             scales = work.tile([P, 2, 2, P], U8, name="scales", align_bytes=64)
             for a in range(2):
                 k_onto_partitions(
                     nc, banks, ident,
-                    got["e_gen1"][:].bitcast(F32)[:, a, :],
-                    got["e_disc3"][:].bitcast(F32)[:, a, :],
-                    grouped[:].bitcast(F32)[:, a], nc.scalar.copy,
+                    loaded[("e_gen1", pair)][:].bitcast(F32)[:, a, :],
+                    loaded[("e_disc3", pair)][:].bitcast(F32)[:, a, :],
+                    grouped[:].bitcast(F32)[:, a],
                 )
             nc.vector.quantize_mx(
                 out=codes[:].rearrange("p a o r -> p (a o r)").bitcast(FP8X4),
                 scales=scales[:].rearrange("p a o r -> p (a o r)"),
                 in_=grouped[:].rearrange("p a o r j -> p (a o r j)"),
             )
+            return codes, scales
 
-            j_kept = work.tile([P, 2, NEURONS], F32, name="j_kept")
-            nc.scalar.mul(out=j_kept[:], in_=got["j2"][:], mul=J_KEEP)
+        def update(pair, codes, scales):
             v_kept = work.tile([P, 2, NEURONS], F32, name="v_kept")
-            nc.scalar.mul(out=v_kept[:], in_=got["v2"][:], mul=V_KEEP)
-            own_err = work.tile([P, 2, NEURONS], F32, name="own_err")
-            for a in range(2):
-                nc.vector.tensor_tensor(
-                    out=own_err[:, a, :], in0=got["e_gen2"][:, a, :],
-                    in1=got["e_disc2"][:, a, :], op=ALU.add,
-                )
-            rest = work.tile([P, 2, NEURONS], F32, name="rest")
-            for a in range(2):
-                nc.vector.scalar_tensor_tensor(
-                    out=rest[:, a, :], in0=own_err[:, a, :], scalar=-J_GAIN,
-                    in1=j_kept[:, a, :], op0=ALU.mult, op1=ALU.add,
-                )
+            nc.scalar.mul(out=v_kept[:], in_=loaded[("v2", pair)][:], mul=V_KEEP)
 
             fed_back = []
             for a in range(2):
@@ -169,7 +172,7 @@ def tile_bspncn_pb_kernel(
             for a in range(2):
                 nc.vector.scalar_tensor_tensor(
                     out=res[a][:, J_COLS], in0=fed_back[a][:], scalar=J_GAIN,
-                    in1=rest[:, a, :], op0=ALU.mult, op1=ALU.add,
+                    in1=rest[pair][:, a, :], op0=ALU.mult, op1=ALU.add,
                 )
             for a in range(2):
                 nc.vector.scalar_tensor_tensor(
@@ -192,7 +195,7 @@ def tile_bspncn_pb_kernel(
                 )
             for a in range(2):
                 nc.vector.scalar_tensor_tensor(
-                    out=res[a][:, X_COLS], in0=got["x2"][:, a, :], scalar=X_KEEP,
+                    out=res[a][:, X_COLS], in0=loaded[("x2", pair)][:, a, :], scalar=X_KEEP,
                     in1=res[a][:, S_COLS], op0=ALU.mult, op1=ALU.add,
                 )
             for a in range(2):
@@ -200,3 +203,9 @@ def tile_bspncn_pb_kernel(
                     out=by_tile(out)[:, 2 * pair + a, 2 * NEURONS : 4 * NEURONS],
                     in_=res[a][:, 2 * NEURONS : 4 * NEURONS],
                 )
+
+        quantised = [quantise_streams(0)]
+        for pair in range(PAIRS):
+            if pair + 1 < PAIRS:
+                quantised.append(quantise_streams(pair + 1))
+            update(pair, quantised[pair][0], quantised[pair][1])

@@ -15,10 +15,11 @@ BATCH = 1024
 NEURONS = 512
 K = 512
 TILES = BATCH // P
-PAIRS = TILES // 2
+GROUP = 4
+GROUPS = TILES // GROUP
 PACK = 4
 WORDS = K // 2
-HALVES = WORDS // P
+WORD_HALVES = WORDS // P
 W_BLOCKS = NEURONS // P
 
 FLOPS = 2 * 2 * BATCH * NEURONS * K
@@ -46,9 +47,9 @@ def by_tile(dram):
 
 
 def k_onto_partitions(nc, banks, ident, block_a, block_b, grouped_words):
-    turned = banks.tile([P, 2, HALVES, P], F32, name="turned")
+    turned = banks.tile([P, 2, WORD_HALVES, P], F32, name="turned")
     for i, block in enumerate((block_a, block_b)):
-        for u in range(HALVES):
+        for u in range(WORD_HALVES):
             nc.tensor.transpose(turned[:, i, u, :], block[:, u * P : (u + 1) * P], ident[:])
     nc.scalar.copy(out=grouped_words, in_=turned[:].rearrange("p i u r -> p i r u"))
 
@@ -60,8 +61,9 @@ def tile_bspncn_pb_kernel(
     with ExitStack() as ctx:
         ctx.enter_context(tc.manual_schedule())
         const = ctx.enter_context(tc.tile_pool(name="const", bufs=1))
-        inputs = ctx.enter_context(tc.tile_pool(name="inputs", bufs=PAIRS))
+        inputs = ctx.enter_context(tc.tile_pool(name="inputs", bufs=GROUPS))
         work = ctx.enter_context(tc.tile_pool(name="work", bufs=2))
+        streams = ctx.enter_context(tc.tile_pool(name="streams", bufs=4))
         results = ctx.enter_context(tc.tile_pool(name="results", bufs=TILES))
         banks = ctx.enter_context(tc.psum_pool(name="banks", bufs=4))
         sums = ctx.enter_context(tc.psum_pool(name="sums", bufs=4))
@@ -75,42 +77,45 @@ def tile_bspncn_pb_kernel(
         }
         loaded = {}
 
-        def load(names, pair):
+        def load(names, g):
             for name in names:
-                sbuf = inputs.tile([P, 2, NEURONS], BF16, name=name)
+                sbuf = inputs.tile([P, GROUP, NEURONS], BF16, name=name)
                 nc.sync.dma_start(
-                    out=sbuf[:], in_=by_tile(sources[name])[:, 2 * pair : 2 * pair + 2, :]
+                    out=sbuf[:], in_=by_tile(sources[name])[:, g * GROUP : (g + 1) * GROUP, :]
                 )
-                loaded[(name, pair)] = sbuf
+                loaded[(name, g)] = sbuf
 
-        for pair in range(PAIRS):
-            load(("j2", "e_gen2", "e_disc2"), pair)
+        def tiles_of(name, first, count):
+            return loaded[(name, first // GROUP)][:, first % GROUP : first % GROUP + count, :]
+
+        for g in range(GROUPS):
+            load(("e_gen2", "e_disc2", "j2"), g)
         w_raw = []
         for o, w in enumerate((Eg1, Ed2)):
             raw = const.tile([P, W_BLOCKS, K], BF16, name="w_raw%d" % o)
             nc.sync.dma_start(out=raw[:], in_=w.rearrange("(r p) k -> p r k", p=P))
             w_raw.append(raw)
-        load(("e_gen1", "e_disc3"), 0)
-        for pair in range(PAIRS):
-            if pair + 1 < PAIRS:
-                load(("e_gen1", "e_disc3"), pair + 1)
-            load(("v2", "x2"), pair)
+        for g in range(GROUPS):
+            load(("e_gen1", "e_disc3", "v2", "x2"), g)
 
         rest = []
-        for pair in range(PAIRS):
-            j_kept = work.tile([P, 2, NEURONS], F32, name="j_kept")
-            nc.scalar.mul(out=j_kept[:], in_=loaded[("j2", pair)][:], mul=J_KEEP)
-            own_err = work.tile([P, 2, NEURONS], F32, name="own_err")
-            for a in range(2):
-                nc.vector.tensor_tensor(
-                    out=own_err[:, a, :], in0=loaded[("e_gen2", pair)][:, a, :],
-                    in1=loaded[("e_disc2", pair)][:, a, :], op=ALU.add,
+        for g in range(GROUPS):
+            j_kept = work.tile([P, GROUP, NEURONS], F32, name="j_kept")
+            for i in range(0, GROUP, 2):
+                nc.scalar.mul(
+                    out=j_kept[:, i : i + 2, :], in_=loaded[("j2", g)][:, i : i + 2, :], mul=J_KEEP
                 )
-            rest.append(inputs.tile([P, 2, NEURONS], F32, name="rest"))
-            for a in range(2):
+            own_err = const.tile([P, GROUP, NEURONS], F32, name="own_err")
+            for i in range(GROUP):
+                nc.vector.tensor_tensor(
+                    out=own_err[:, i, :], in0=loaded[("e_gen2", g)][:, i, :],
+                    in1=loaded[("e_disc2", g)][:, i, :], op=ALU.add,
+                )
+            rest.append(inputs.tile([P, GROUP, NEURONS], F32, name="rest"))
+            for i in range(GROUP):
                 nc.vector.scalar_tensor_tensor(
-                    out=rest[pair][:, a, :], in0=own_err[:, a, :], scalar=-J_GAIN,
-                    in1=j_kept[:, a, :], op0=ALU.mult, op1=ALU.add,
+                    out=rest[g][:, i, :], in0=own_err[:, i, :], scalar=-J_GAIN,
+                    in1=j_kept[:, i, :], op0=ALU.mult, op1=ALU.add,
                 )
 
         w_grouped = const.tile([P, 2, W_BLOCKS, P, PACK], BF16, name="w_grouped", align_bytes=64)
@@ -130,36 +135,38 @@ def tile_bspncn_pb_kernel(
                 in_=w_grouped[:, o].rearrange("p r c j -> p (r c j)"),
             )
 
-        def quantise_streams(pair):
-            grouped = work.tile([P, 2, 2, P, PACK], BF16, name="grouped", align_bytes=64)
-            codes = work.tile([P, 2, 2, P], U32, name="codes", align_bytes=64)
-            scales = work.tile([P, 2, 2, P], U8, name="scales", align_bytes=64)
-            for a in range(2):
-                k_onto_partitions(
-                    nc, banks, ident,
-                    loaded[("e_gen1", pair)][:].bitcast(F32)[:, a, :],
-                    loaded[("e_disc3", pair)][:].bitcast(F32)[:, a, :],
-                    grouped[:].bitcast(F32)[:, a],
-                )
+        def quantise_streams(t):
+            grouped = streams.tile([P, 2, P, PACK], BF16, name="grouped", align_bytes=64)
+            codes = streams.tile([P, 2, P], U32, name="codes", align_bytes=64)
+            scales = streams.tile([P, 2, P], U8, name="scales", align_bytes=64)
+            k_onto_partitions(
+                nc, banks, ident,
+                tiles_of("e_gen1", t, 1).bitcast(F32)[:, 0, :],
+                tiles_of("e_disc3", t, 1).bitcast(F32)[:, 0, :],
+                grouped[:].bitcast(F32),
+            )
             nc.vector.quantize_mx(
-                out=codes[:].rearrange("p a o r -> p (a o r)").bitcast(FP8X4),
-                scales=scales[:].rearrange("p a o r -> p (a o r)"),
-                in_=grouped[:].rearrange("p a o r j -> p (a o r j)"),
+                out=codes[:].rearrange("p o r -> p (o r)").bitcast(FP8X4),
+                scales=scales[:].rearrange("p o r -> p (o r)"),
+                in_=grouped[:].rearrange("p o r j -> p (o r j)"),
             )
             return codes, scales
 
-        def update(pair, codes, scales):
+        def update(first, quantised):
             v_kept = work.tile([P, 2, NEURONS], F32, name="v_kept")
-            nc.scalar.mul(out=v_kept[:], in_=loaded[("v2", pair)][:], mul=V_KEEP)
+            nc.scalar.mul(out=v_kept[:], in_=tiles_of("v2", first, 2), mul=V_KEEP)
+            pair_rest = rest[first // GROUP][:, first % GROUP : first % GROUP + 2, :]
+            pair_x2 = tiles_of("x2", first, 2)
 
             fed_back = []
             for a in range(2):
+                codes, scales = quantised[a]
                 acc = sums.tile([P, NEURONS], F32, name="acc")
                 for o in range(2):
                     nc.tensor.matmul_mx(
                         out=acc[:],
-                        lhsT=codes[:, a, o, :].bitcast(FP8X4),
-                        lhsT_scale=scales[:, a, o, :],
+                        lhsT=codes[:, o, :].bitcast(FP8X4),
+                        lhsT_scale=scales[:, o, :],
                         rhs=w_codes[:, o, :].bitcast(FP8X4),
                         rhs_scale=w_scales[:, o, :],
                         start=(o == 0),
@@ -172,7 +179,7 @@ def tile_bspncn_pb_kernel(
             for a in range(2):
                 nc.vector.scalar_tensor_tensor(
                     out=res[a][:, J_COLS], in0=fed_back[a][:], scalar=J_GAIN,
-                    in1=rest[pair][:, a, :], op0=ALU.mult, op1=ALU.add,
+                    in1=pair_rest[:, a, :], op0=ALU.mult, op1=ALU.add,
                 )
             for a in range(2):
                 nc.vector.scalar_tensor_tensor(
@@ -186,7 +193,7 @@ def tile_bspncn_pb_kernel(
                 )
             for a in range(2):
                 nc.sync.dma_start(
-                    out=by_tile(out)[:, 2 * pair + a, 0 : 2 * NEURONS],
+                    out=by_tile(out)[:, first + a, 0 : 2 * NEURONS],
                     in_=res[a][:, 0 : 2 * NEURONS],
                 )
             for a in range(2):
@@ -195,17 +202,18 @@ def tile_bspncn_pb_kernel(
                 )
             for a in range(2):
                 nc.vector.scalar_tensor_tensor(
-                    out=res[a][:, X_COLS], in0=loaded[("x2", pair)][:, a, :], scalar=X_KEEP,
+                    out=res[a][:, X_COLS], in0=pair_x2[:, a, :], scalar=X_KEEP,
                     in1=res[a][:, S_COLS], op0=ALU.mult, op1=ALU.add,
                 )
             for a in range(2):
                 nc.sync.dma_start(
-                    out=by_tile(out)[:, 2 * pair + a, 2 * NEURONS : 4 * NEURONS],
+                    out=by_tile(out)[:, first + a, 2 * NEURONS : 4 * NEURONS],
                     in_=res[a][:, 2 * NEURONS : 4 * NEURONS],
                 )
 
-        quantised = [quantise_streams(0)]
-        for pair in range(PAIRS):
-            if pair + 1 < PAIRS:
-                quantised.append(quantise_streams(pair + 1))
-            update(pair, quantised[pair][0], quantised[pair][1])
+        quantised = [quantise_streams(0), quantise_streams(1)]
+        for first in range(0, TILES, 2):
+            if first + 2 < TILES:
+                quantised.append(quantise_streams(first + 2))
+                quantised.append(quantise_streams(first + 3))
+            update(first, quantised[first : first + 2])

@@ -9,14 +9,13 @@ U32 = mybir.dt.uint32
 U8 = mybir.dt.uint8
 FP8X4 = mybir.dt.float8_e4m3fn_x4
 ALU = mybir.AluOpType
+ACT = mybir.ActivationFunctionType
 
 P = 128
 BATCH = 1024
 NEURONS = 512
 K = 512
 TILES = BATCH // P
-GROUP = 4
-GROUPS = TILES // GROUP
 PACK = 4
 WORDS = K // 2
 WORD_HALVES = WORDS // P
@@ -61,10 +60,14 @@ def tile_bspncn_pb_kernel(
     with ExitStack() as ctx:
         ctx.enter_context(tc.manual_schedule())
         const = ctx.enter_context(tc.tile_pool(name="const", bufs=1))
-        inputs = ctx.enter_context(tc.tile_pool(name="inputs", bufs=GROUPS))
-        work = ctx.enter_context(tc.tile_pool(name="work", bufs=2))
+        inputs = ctx.enter_context(tc.tile_pool(name="inputs", bufs=1))
+        head = ctx.enter_context(tc.tile_pool(name="head", bufs=2))
+        rests = ctx.enter_context(tc.tile_pool(name="rests", bufs=TILES // 2))
+        work = ctx.enter_context(tc.tile_pool(name="work", bufs=3))
+        ahead = ctx.enter_context(tc.tile_pool(name="ahead", bufs=4))
+        turned_pool = ctx.enter_context(tc.tile_pool(name="turned_pool", bufs=6))
         streams = ctx.enter_context(tc.tile_pool(name="streams", bufs=4))
-        results = ctx.enter_context(tc.tile_pool(name="results", bufs=TILES))
+        results = ctx.enter_context(tc.tile_pool(name="results", bufs=6))
         banks = ctx.enter_context(tc.psum_pool(name="banks", bufs=4))
         sums = ctx.enter_context(tc.psum_pool(name="sums", bufs=4))
 
@@ -75,76 +78,99 @@ def tile_bspncn_pb_kernel(
             "e_gen2": e_gen2, "e_disc2": e_disc2, "e_gen1": e_gen1, "e_disc3": e_disc3,
             "j2": j2, "v2": v2, "x2": x2,
         }
-        loaded = {}
+        where = {}
 
-        def load(names, g):
+        def load(names, first, count):
             for name in names:
-                sbuf = inputs.tile([P, GROUP, NEURONS], BF16, name=name)
-                nc.sync.dma_start(
-                    out=sbuf[:], in_=by_tile(sources[name])[:, g * GROUP : (g + 1) * GROUP, :]
-                )
-                loaded[(name, g)] = sbuf
+                sbuf = inputs.tile([P, count, NEURONS], BF16, name="%s_%d" % (name, first))
+                nc.sync.dma_start(out=sbuf[:], in_=by_tile(sources[name])[:, first : first + count, :])
+                for t in range(first, first + count):
+                    where[(name, t)] = (sbuf, t - first)
 
         def tiles_of(name, first, count):
-            return loaded[(name, first // GROUP)][:, first % GROUP : first % GROUP + count, :]
+            sbuf, i = where[(name, first)]
+            return sbuf[:, i : i + count, :]
 
-        for g in range(GROUPS):
-            load(("e_gen2", "e_disc2", "j2"), g)
         w_raw = []
-        for o, w in enumerate((Eg1, Ed2)):
-            raw = const.tile([P, W_BLOCKS, K], BF16, name="w_raw%d" % o)
+
+        def load_weights(w):
+            raw = const.tile([P, W_BLOCKS, K], BF16, name="w_raw%d" % len(w_raw))
             nc.sync.dma_start(out=raw[:], in_=w.rearrange("(r p) k -> p r k", p=P))
             w_raw.append(raw)
-        for g in range(GROUPS):
-            load(("e_gen1", "e_disc3", "v2", "x2"), g)
+
+        own = ("e_gen2", "e_disc2", "j2")
+        load(own, 0, 1)
+        load(own, 1, 1)
+        own = ("j2", "e_gen2", "e_disc2")
+        load(own, 2, 2)
+        load_weights(Eg1)
+        load(own, 4, 2)
+        load_weights(Ed2)
+        load(own, 6, 2)
+        load(("e_gen1", "e_disc3", "v2"), 0, 2)
+        load(("e_gen1", "e_disc3"), 2, 2)
+        load(("x2",), 0, 2)
+        load(("v2",), 2, 2)
+        load(("e_gen1", "e_disc3"), 4, 2)
+        load(("x2",), 2, 2)
+        load(("e_gen1", "e_disc3"), 6, 2)
+        load(("v2", "x2"), 4, 4)
 
         rest = []
-        for g in range(GROUPS):
-            j_kept = work.tile([P, GROUP, NEURONS], F32, name="j_kept")
-            for i in range(0, GROUP, 2):
-                nc.scalar.mul(
-                    out=j_kept[:, i : i + 2, :], in_=loaded[("j2", g)][:, i : i + 2, :], mul=J_KEEP
-                )
-            own_err = const.tile([P, GROUP, NEURONS], F32, name="own_err")
-            for i in range(GROUP):
+
+        def own_errors(first, chunks):
+            j_kept = head.tile([P, 2, NEURONS], F32, name="j_kept")
+            own_err = head.tile([P, 2, NEURONS], F32, name="own_err")
+            step = 2 // chunks
+            for a in range(0, 2, step):
+                nc.scalar.mul(out=j_kept[:, a : a + step, :], in_=tiles_of("j2", first + a, step), mul=J_KEEP)
+            for a in range(2):
                 nc.vector.tensor_tensor(
-                    out=own_err[:, i, :], in0=loaded[("e_gen2", g)][:, i, :],
-                    in1=loaded[("e_disc2", g)][:, i, :], op=ALU.add,
+                    out=own_err[:, a, :], in0=tiles_of("e_gen2", first + a, 1)[:, 0, :],
+                    in1=tiles_of("e_disc2", first + a, 1)[:, 0, :], op=ALU.add,
                 )
-            rest.append(inputs.tile([P, GROUP, NEURONS], F32, name="rest"))
-            for i in range(GROUP):
-                nc.vector.scalar_tensor_tensor(
-                    out=rest[g][:, i, :], in0=own_err[:, i, :], scalar=-J_GAIN,
-                    in1=j_kept[:, i, :], op0=ALU.mult, op1=ALU.add,
-                )
+            rest.append(rests.tile([P, 2, NEURONS], F32, name="rest"))
+            return j_kept, own_err
+
+        def product_free(t, parts):
+            j_kept, own_err = parts
+            nc.vector.scalar_tensor_tensor(
+                out=rest[t // 2][:, t % 2, :], in0=own_err[:, t % 2, :], scalar=-J_GAIN,
+                in1=j_kept[:, t % 2, :], op0=ALU.mult, op1=ALU.add,
+            )
 
         w_grouped = const.tile([P, 2, W_BLOCKS, P, PACK], BF16, name="w_grouped", align_bytes=64)
         w_codes = const.tile([P, 2, NEURONS], U32, name="w_codes", align_bytes=64)
         w_scales = const.tile([P, 2, NEURONS], U8, name="w_scales", align_bytes=64)
-        for o in range(2):
+
+        def turn_weights(o):
             raw_words = w_raw[o][:].bitcast(F32)
             for r in range(0, W_BLOCKS, 2):
                 k_onto_partitions(
                     nc, banks, ident, raw_words[:, r, :], raw_words[:, r + 1, :],
                     w_grouped[:].bitcast(F32)[:, o, r : r + 2],
                 )
-        for o in range(2):
+
+        def quantise_weights(o):
             nc.vector.quantize_mx(
                 out=w_codes[:, o, :].bitcast(FP8X4),
                 scales=w_scales[:, o, :],
                 in_=w_grouped[:, o].rearrange("p r c j -> p (r c j)"),
             )
 
-        def quantise_streams(t):
-            grouped = streams.tile([P, 2, P, PACK], BF16, name="grouped", align_bytes=64)
-            codes = streams.tile([P, 2, P], U32, name="codes", align_bytes=64)
-            scales = streams.tile([P, 2, P], U8, name="scales", align_bytes=64)
+        def turn_streams(t):
+            grouped = turned_pool.tile([P, 2, P, PACK], BF16, name="grouped", align_bytes=64)
             k_onto_partitions(
                 nc, banks, ident,
                 tiles_of("e_gen1", t, 1).bitcast(F32)[:, 0, :],
                 tiles_of("e_disc3", t, 1).bitcast(F32)[:, 0, :],
                 grouped[:].bitcast(F32),
             )
+            return grouped
+
+        def quantise_streams(grouped):
+            codes = streams.tile([P, 2, P], U32, name="codes", align_bytes=64)
+            scales = streams.tile([P, 2, P], U8, name="scales", align_bytes=64)
             nc.vector.quantize_mx(
                 out=codes[:].rearrange("p o r -> p (o r)").bitcast(FP8X4),
                 scales=scales[:].rearrange("p o r -> p (o r)"),
@@ -152,68 +178,130 @@ def tile_bspncn_pb_kernel(
             )
             return codes, scales
 
-        def update(first, quantised):
-            v_kept = work.tile([P, 2, NEURONS], F32, name="v_kept")
-            nc.scalar.mul(out=v_kept[:], in_=tiles_of("v2", first, 2), mul=V_KEEP)
-            pair_rest = rest[first // GROUP][:, first % GROUP : first % GROUP + 2, :]
-            pair_x2 = tiles_of("x2", first, 2)
+        def keep_potential(t):
+            v_kept = ahead.tile([P, NEURONS], F32, name="v_kept")
+            nc.scalar.mul(out=v_kept[:], in_=tiles_of("v2", t, 1)[:, 0, :], mul=V_KEEP)
+            return v_kept
 
-            fed_back = []
-            for a in range(2):
-                codes, scales = quantised[a]
-                acc = sums.tile([P, NEURONS], F32, name="acc")
-                for o in range(2):
-                    nc.tensor.matmul_mx(
-                        out=acc[:],
-                        lhsT=codes[:, o, :].bitcast(FP8X4),
-                        lhsT_scale=scales[:, o, :],
-                        rhs=w_codes[:, o, :].bitcast(FP8X4),
-                        rhs_scale=w_scales[:, o, :],
-                        start=(o == 0),
-                        stop=(o == 1),
-                    )
-                fed_back.append(acc)
+        def multiply(codes, scales):
+            acc = sums.tile([P, NEURONS], F32, name="acc")
+            for o in range(2):
+                nc.tensor.matmul_mx(
+                    out=acc[:],
+                    lhsT=codes[:, o, :].bitcast(FP8X4),
+                    lhsT_scale=scales[:, o, :],
+                    rhs=w_codes[:, o, :].bitcast(FP8X4),
+                    rhs_scale=w_scales[:, o, :],
+                    start=(o == 0),
+                    stop=(o == 1),
+                )
+            return acc
 
-            res = [results.tile([P, 4 * NEURONS], F32, name="res") for a in range(2)]
-            v_pre = work.tile([P, 2, NEURONS], F32, name="v_pre")
-            for a in range(2):
-                nc.vector.scalar_tensor_tensor(
-                    out=res[a][:, J_COLS], in0=fed_back[a][:], scalar=J_GAIN,
-                    in1=pair_rest[:, a, :], op0=ALU.mult, op1=ALU.add,
-                )
-            for a in range(2):
-                nc.vector.scalar_tensor_tensor(
-                    out=v_pre[:, a, :], in0=res[a][:, J_COLS], scalar=V_GAIN,
-                    in1=v_kept[:, a, :], op0=ALU.mult, op1=ALU.add,
-                )
-            for a in range(2):
-                nc.vector.scalar_tensor_tensor(
-                    out=res[a][:, V_COLS], in0=v_pre[:, a, :], scalar=THRESH,
-                    in1=v_pre[:, a, :], op0=ALU.is_le, op1=ALU.mult,
-                )
-            for a in range(2):
-                nc.sync.dma_start(
-                    out=by_tile(out)[:, first + a, 0 : 2 * NEURONS],
-                    in_=res[a][:, 0 : 2 * NEURONS],
-                )
-            for a in range(2):
-                nc.vector.tensor_single_scalar(
-                    out=res[a][:, S_COLS], in_=v_pre[:, a, :], scalar=THRESH, op=ALU.is_gt
-                )
-            for a in range(2):
-                nc.vector.scalar_tensor_tensor(
-                    out=res[a][:, X_COLS], in0=pair_x2[:, a, :], scalar=X_KEEP,
-                    in1=res[a][:, S_COLS], op0=ALU.mult, op1=ALU.add,
-                )
-            for a in range(2):
-                nc.sync.dma_start(
-                    out=by_tile(out)[:, first + a, 2 * NEURONS : 4 * NEURONS],
-                    in_=res[a][:, 2 * NEURONS : 4 * NEURONS],
-                )
+        res = {}
+        v_pre = {}
+        turned = {}
+        quantised = {}
+        fed_back = {}
+        v_kept = {}
 
-        quantised = [quantise_streams(0), quantise_streams(1)]
-        for first in range(0, TILES, 2):
-            if first + 2 < TILES:
-                quantised.append(quantise_streams(first + 2))
-                quantised.append(quantise_streams(first + 3))
-            update(first, quantised[first : first + 2])
+        def current(t):
+            res[t] = results.tile([P, 4 * NEURONS], F32, name="res")
+            nc.vector.scalar_tensor_tensor(
+                out=res[t][:, J_COLS], in0=fed_back[t][:], scalar=J_GAIN,
+                in1=rest[t // 2][:, t % 2, :], op0=ALU.mult, op1=ALU.add,
+            )
+            nc.sync.dma_start(out=by_tile(out)[:, t, J_COLS], in_=res[t][:, J_COLS])
+
+        def potential(t):
+            v_pre[t] = work.tile([P, NEURONS], F32, name="v_pre")
+            nc.vector.scalar_tensor_tensor(
+                out=v_pre[t][:], in0=res[t][:, J_COLS], scalar=V_GAIN,
+                in1=v_kept[t][:], op0=ALU.mult, op1=ALU.add,
+            )
+
+        def spikes(t):
+            sgn = work.tile([P, NEURONS], F32, name="sgn")
+            nc.scalar.activation(out=sgn[:], in_=v_pre[t][:], func=ACT.Sign, bias=-THRESH, scale=1.0)
+            nc.scalar.activation(out=res[t][:, S_COLS], in_=sgn[:], func=ACT.Relu)
+
+        def reset(t):
+            nc.vector.scalar_tensor_tensor(
+                out=res[t][:, V_COLS], in0=v_pre[t][:], scalar=THRESH,
+                in1=v_pre[t][:], op0=ALU.is_le, op1=ALU.mult,
+            )
+            nc.sync.dma_start(out=by_tile(out)[:, t, V_COLS], in_=res[t][:, V_COLS])
+
+        def trace(t):
+            nc.vector.scalar_tensor_tensor(
+                out=res[t][:, X_COLS], in0=tiles_of("x2", t, 1)[:, 0, :], scalar=X_KEEP,
+                in1=res[t][:, S_COLS], op0=ALU.mult, op1=ALU.add,
+            )
+            nc.sync.dma_start(
+                out=by_tile(out)[:, t, 2 * NEURONS : 4 * NEURONS], in_=res[t][:, 2 * NEURONS : 4 * NEURONS]
+            )
+
+        def keep_trace(t):
+            x_kept = const.tile([P, NEURONS], F32, name="x_kept")
+            nc.scalar.mul(out=x_kept[:], in_=tiles_of("x2", t, 1)[:, 0, :], mul=X_KEEP)
+            return x_kept
+
+        def last_trace(t, x_kept):
+            nc.sync.dma_start(out=by_tile(out)[:, t, S_COLS], in_=res[t][:, S_COLS])
+            nc.vector.scalar_tensor_tensor(
+                out=res[t][:, X_COLS], in0=v_pre[t][:], scalar=THRESH,
+                in1=x_kept[:], op0=ALU.is_gt, op1=ALU.add,
+            )
+            nc.sync.dma_start(out=by_tile(out)[:, t, X_COLS], in_=res[t][:, X_COLS])
+
+        parts = own_errors(0, 2)
+        product_free(0, parts)
+        product_free(1, parts)
+        parts = own_errors(2, 1)
+        product_free(2, parts)
+        product_free(3, parts)
+        turn_weights(0)
+        parts = own_errors(4, 1)
+        product_free(4, parts)
+        product_free(5, parts)
+        quantise_weights(0)
+        turn_weights(1)
+        parts = own_errors(6, 1)
+        for t in range(3):
+            turned[t] = turn_streams(t)
+        quantise_weights(1)
+        quantised[0] = quantise_streams(turned[0])
+        product_free(6, parts)
+        quantised[1] = quantise_streams(turned[1])
+        fed_back[0] = multiply(*quantised[0])
+        fed_back[1] = multiply(*quantised[1])
+        for t in range(2):
+            v_kept[t] = keep_potential(t)
+        turned[3] = turn_streams(3)
+        product_free(7, parts)
+        current(0)
+        quantised[2] = quantise_streams(turned[2])
+        potential(0)
+        spikes(0)
+        v_kept[2] = keep_potential(2)
+
+        for t in range(TILES):
+            if t + 2 < TILES:
+                fed_back[t + 2] = multiply(*quantised[t + 2])
+            if t + 1 < TILES:
+                current(t + 1)
+            reset(t)
+            if t + 1 < TILES:
+                potential(t + 1)
+                spikes(t + 1)
+            if t + 3 < TILES:
+                v_kept[t + 3] = keep_potential(t + 3)
+            if t + 4 < TILES:
+                turned[t + 4] = turn_streams(t + 4)
+            if t + 3 == TILES:
+                x_kept = keep_trace(TILES - 1)
+            if t + 1 < TILES:
+                trace(t)
+            else:
+                last_trace(t, x_kept)
+            if t + 3 < TILES:
+                quantised[t + 3] = quantise_streams(turned[t + 3])

@@ -45,12 +45,12 @@ def by_tile(dram):
     return dram.rearrange("(p t) c -> p t c", t=TILES)
 
 
-def k_onto_partitions(nc, banks, ident, block_a, block_b, grouped_words):
+def k_onto_partitions(nc, banks, ident, block_a, block_b, grouped_words, order):
     turned = banks.tile([P, 2, WORD_HALVES, P], F32, name="turned")
     for i, block in enumerate((block_a, block_b)):
         for u in range(WORD_HALVES):
             nc.tensor.transpose(turned[:, i, u, :], block[:, u * P : (u + 1) * P], ident[:])
-    nc.scalar.copy(out=grouped_words, in_=turned[:].rearrange("p i u r -> p i r u"))
+    nc.scalar.copy(out=grouped_words, in_=turned[:].rearrange("p i u r -> " + order))
 
 
 def tile_bspncn_pb_kernel(
@@ -95,7 +95,7 @@ def tile_bspncn_pb_kernel(
 
         def load_weights(w):
             raw = const.tile([P, W_BLOCKS, K], BF16, name="w_raw%d" % len(w_raw))
-            nc.sync.dma_start(out=raw[:], in_=w.rearrange("(r p) k -> p r k", p=P))
+            nc.sync.dma_start(out=raw[:], in_=w.rearrange("(p r) k -> p r k", r=W_BLOCKS))
             w_raw.append(raw)
 
         own = ("e_gen2", "e_disc2", "j2")
@@ -107,14 +107,10 @@ def tile_bspncn_pb_kernel(
         load(own, 4, 2)
         load_weights(Ed2)
         load(own, 6, 2)
-        load(("e_gen1", "e_disc3", "v2"), 0, 2)
+        load(("e_gen1", "e_disc3"), 0, 2)
         load(("e_gen1", "e_disc3"), 2, 2)
-        load(("x2",), 0, 2)
-        load(("v2",), 2, 2)
-        load(("e_gen1", "e_disc3"), 4, 2)
-        load(("x2",), 2, 2)
-        load(("e_gen1", "e_disc3"), 6, 2)
-        load(("v2", "x2"), 4, 4)
+        load(("v2", "x2"), 0, 4)
+        load(("e_gen1", "e_disc3", "v2", "x2"), 4, 4)
 
         rest = []
 
@@ -139,7 +135,7 @@ def tile_bspncn_pb_kernel(
                 in1=j_kept[:, t % 2, :], op0=ALU.mult, op1=ALU.add,
             )
 
-        w_grouped = const.tile([P, 2, W_BLOCKS, P, PACK], BF16, name="w_grouped", align_bytes=64)
+        w_grouped = const.tile([P, 2, NEURONS, PACK], BF16, name="w_grouped", align_bytes=64)
         w_codes = const.tile([P, 2, NEURONS], U32, name="w_codes", align_bytes=64)
         w_scales = const.tile([P, 2, NEURONS], U8, name="w_scales", align_bytes=64)
 
@@ -148,14 +144,15 @@ def tile_bspncn_pb_kernel(
             for r in range(0, W_BLOCKS, 2):
                 k_onto_partitions(
                     nc, banks, ident, raw_words[:, r, :], raw_words[:, r + 1, :],
-                    w_grouped[:].bitcast(F32)[:, o, r : r + 2],
+                    w_grouped[:].bitcast(F32)[:, o].rearrange("q (p r) u -> q p r u", r=W_BLOCKS)[:, :, r : r + 2, :],
+                    "p r i u",
                 )
 
         def quantise_weights(o):
             nc.vector.quantize_mx(
                 out=w_codes[:, o, :].bitcast(FP8X4),
                 scales=w_scales[:, o, :],
-                in_=w_grouped[:, o].rearrange("p r c j -> p (r c j)"),
+                in_=w_grouped[:, o].rearrange("p n j -> p (n j)"),
             )
 
         def turn_streams(t):
@@ -165,6 +162,7 @@ def tile_bspncn_pb_kernel(
                 tiles_of("e_gen1", t, 1).bitcast(F32)[:, 0, :],
                 tiles_of("e_disc3", t, 1).bitcast(F32)[:, 0, :],
                 grouped[:].bitcast(F32),
+                "p i r u",
             )
             return grouped
 
@@ -210,7 +208,8 @@ def tile_bspncn_pb_kernel(
                 out=res[t][:, J_COLS], in0=fed_back[t][:], scalar=J_GAIN,
                 in1=rest[t // 2][:, t % 2, :], op0=ALU.mult, op1=ALU.add,
             )
-            nc.sync.dma_start(out=by_tile(out)[:, t, J_COLS], in_=res[t][:, J_COLS])
+            if t >= TILES - 2:
+                nc.sync.dma_start(out=by_tile(out)[:, t, J_COLS], in_=res[t][:, J_COLS])
 
         def potential(t):
             v_pre[t] = work.tile([P, NEURONS], F32, name="v_pre")
@@ -229,7 +228,8 @@ def tile_bspncn_pb_kernel(
                 out=res[t][:, V_COLS], in0=v_pre[t][:], scalar=THRESH,
                 in1=v_pre[t][:], op0=ALU.is_le, op1=ALU.mult,
             )
-            nc.sync.dma_start(out=by_tile(out)[:, t, V_COLS], in_=res[t][:, V_COLS])
+            cols = V_COLS if t >= TILES - 2 else slice(0, 2 * NEURONS)
+            nc.sync.dma_start(out=by_tile(out)[:, t, cols], in_=res[t][:, cols])
 
         def trace(t):
             nc.vector.scalar_tensor_tensor(

@@ -31,6 +31,7 @@ THRESH = 0.4
 X_DECAY = 20.0
 J_GAIN = DT / TAU_J
 J_KEEP = 1.0 - J_GAIN * KAPPA_J
+J_RATIO = TAU_J / DT - KAPPA_J
 V_GAIN = DT / TAU_M
 V_KEEP = 1.0 - V_GAIN
 X_KEEP = 1.0 - 1.0 / X_DECAY
@@ -73,6 +74,12 @@ def tile_bspncn_pb_kernel(
 
         ident = const.tile([P, P], F32, name="ident")
         make_identity(nc, ident[:])
+        ident_bf = const.tile([P, P], BF16, name="ident_bf")
+        make_identity(nc, ident_bf[:])
+        minus_one = const.tile([P, P], BF16, name="minus_one")
+        nc.scalar.mul(out=minus_one[:], in_=ident_bf[:], mul=-1.0)
+        j_ratio = const.tile([P, P], BF16, name="j_ratio")
+        nc.scalar.mul(out=j_ratio[:], in_=ident_bf[:], mul=J_RATIO)
 
         sources = {
             "e_gen2": e_gen2, "e_disc2": e_disc2, "e_gen1": e_gen1, "e_disc3": e_disc3,
@@ -106,11 +113,11 @@ def tile_bspncn_pb_kernel(
         load_weights(Eg1)
         load(own, 4, 2)
         load_weights(Ed2)
-        load(own, 6, 2)
         load(("e_gen1", "e_disc3"), 0, 2)
         load(("e_gen1", "e_disc3"), 2, 2)
         load(("v2", "x2"), 0, 4)
         load(("e_gen1", "e_disc3", "v2", "x2"), 4, 4)
+        load(own, 6, 2)
 
         rest = []
 
@@ -134,6 +141,19 @@ def tile_bspncn_pb_kernel(
                 out=rest[t // 2][:, t % 2, :], in0=own_err[:, t % 2, :], scalar=-J_GAIN,
                 in1=j_kept[:, t % 2, :], op0=ALU.mult, op1=ALU.add,
             )
+
+        def sum_on_tensor(t):
+            acc = sums.tile([P, NEURONS], F32, name="acc")
+            terms = ((minus_one, "e_gen2"), (minus_one, "e_disc2"), (j_ratio, "j2"))
+            for i, (factor, name) in enumerate(terms):
+                nc.tensor.matmul(
+                    out=acc[:], lhsT=factor[:], rhs=tiles_of(name, t, 1)[:, 0, :],
+                    start=(i == 0), stop=(i == len(terms) - 1),
+                )
+            return acc
+
+        def product_free_from_sum(t, acc):
+            nc.scalar.mul(out=rest[t // 2][:, t % 2, :], in_=acc[:], mul=J_GAIN)
 
         w_grouped = const.tile([P, 2, NEURONS, PACK], BF16, name="w_grouped", align_bytes=64)
         w_codes = const.tile([P, 2, NEURONS], U32, name="w_codes", align_bytes=64)
@@ -259,30 +279,28 @@ def tile_bspncn_pb_kernel(
         parts = own_errors(2, 1)
         product_free(2, parts)
         product_free(3, parts)
-        turn_weights(0)
         parts = own_errors(4, 1)
+        turn_weights(0)
         product_free(4, parts)
         product_free(5, parts)
         quantise_weights(0)
         turn_weights(1)
-        parts = own_errors(6, 1)
         for t in range(3):
             turned[t] = turn_streams(t)
         quantise_weights(1)
         quantised[0] = quantise_streams(turned[0])
-        product_free(6, parts)
         quantised[1] = quantise_streams(turned[1])
         fed_back[0] = multiply(*quantised[0])
         fed_back[1] = multiply(*quantised[1])
         for t in range(2):
             v_kept[t] = keep_potential(t)
         turned[3] = turn_streams(3)
-        product_free(7, parts)
         current(0)
         quantised[2] = quantise_streams(turned[2])
         potential(0)
         spikes(0)
         v_kept[2] = keep_potential(2)
+        rest.append(rests.tile([P, 2, NEURONS], F32, name="rest"))
 
         for t in range(TILES):
             if t + 2 < TILES:
@@ -297,6 +315,11 @@ def tile_bspncn_pb_kernel(
                 v_kept[t + 3] = keep_potential(t + 3)
             if t + 4 < TILES:
                 turned[t + 4] = turn_streams(t + 4)
+            if t == 2:
+                sums_67 = [sum_on_tensor(6), sum_on_tensor(7)]
+            if t == 3:
+                product_free_from_sum(6, sums_67[0])
+                product_free_from_sum(7, sums_67[1])
             if t + 3 == TILES:
                 x_kept = keep_trace(TILES - 1)
             if t + 1 < TILES:

@@ -59,7 +59,6 @@ def tile_bspncn_pb_kernel(
 ):
     nc = tc.nc
     with ExitStack() as ctx:
-        ctx.enter_context(tc.manual_schedule())
         const = ctx.enter_context(tc.tile_pool(name="const", bufs=1))
         inputs = ctx.enter_context(tc.tile_pool(name="inputs", bufs=1))
         head = ctx.enter_context(tc.tile_pool(name="head", bufs=2))

@@ -105,12 +105,10 @@ def tile_bspncn_pb_kernel(
             w_raw.append(raw)
 
         own = ("e_gen2", "e_disc2", "j2")
-        load(own, 0, 1)
-        load(own, 1, 1)
+        load(own, 0, 2)
         own = ("j2", "e_gen2", "e_disc2")
-        load(own, 2, 2)
+        load(own, 2, 4)
         load_weights(Eg1)
-        load(own, 4, 2)
         load_weights(Ed2)
         load(("e_gen1", "e_disc3"), 0, 2)
         load(("e_gen1", "e_disc3"), 2, 2)
@@ -227,8 +225,6 @@ def tile_bspncn_pb_kernel(
                 out=res[t][:, J_COLS], in0=fed_back[t][:], scalar=J_GAIN,
                 in1=rest[t // 2][:, t % 2, :], op0=ALU.mult, op1=ALU.add,
             )
-            if t >= TILES - 2:
-                nc.sync.dma_start(out=by_tile(out)[:, t, J_COLS], in_=res[t][:, J_COLS])
 
         def potential(t):
             v_pre[t] = work.tile([P, NEURONS], F32, name="v_pre")
@@ -247,7 +243,7 @@ def tile_bspncn_pb_kernel(
                 out=res[t][:, V_COLS], in0=v_pre[t][:], scalar=THRESH,
                 in1=v_pre[t][:], op0=ALU.is_le, op1=ALU.mult,
             )
-            cols = V_COLS if t >= TILES - 2 else slice(0, 2 * NEURONS)
+            cols = slice(0, 2 * NEURONS)
             nc.sync.dma_start(out=by_tile(out)[:, t, cols], in_=res[t][:, cols])
 
         def trace(t):
@@ -265,14 +261,15 @@ def tile_bspncn_pb_kernel(
             return x_kept
 
         def last_trace(t, x_kept):
-            nc.sync.dma_start(out=by_tile(out)[:, t, S_COLS], in_=res[t][:, S_COLS])
             nc.vector.scalar_tensor_tensor(
                 out=res[t][:, X_COLS], in0=v_pre[t][:], scalar=THRESH,
                 in1=x_kept[:], op0=ALU.is_gt, op1=ALU.add,
             )
-            nc.sync.dma_start(out=by_tile(out)[:, t, X_COLS], in_=res[t][:, X_COLS])
+            nc.sync.dma_start(
+                out=by_tile(out)[:, t, 2 * NEURONS : 4 * NEURONS], in_=res[t][:, 2 * NEURONS : 4 * NEURONS]
+            )
 
-        parts = own_errors(0, 2)
+        parts = own_errors(0, 1)
         product_free(0, parts)
         product_free(1, parts)
         parts = own_errors(2, 1)

from contextlib import ExitStack

import concourse.mybir as mybir
from concourse.masks import make_identity

F32 = mybir.dt.float32
BF16 = mybir.dt.bfloat16
U32 = mybir.dt.uint32
U8 = mybir.dt.uint8
FP8X4 = mybir.dt.float8_e4m3fn_x4
ALU = mybir.AluOpType
ACT = mybir.ActivationFunctionType

P = 128
BATCH = 1024
NEURONS = 512
K = 512
TILES = BATCH // P
PACK = 4
WORDS = K // 2
WORD_HALVES = WORDS // P
W_BLOCKS = NEURONS // P

FLOPS = 2 * 2 * BATCH * NEURONS * K

DT = 1.0
TAU_J = 10.0
TAU_M = 20.0
KAPPA_J = 0.25
THRESH = 0.4
X_DECAY = 20.0
J_GAIN = DT / TAU_J
J_KEEP = 1.0 - J_GAIN * KAPPA_J
J_RATIO = TAU_J / DT - KAPPA_J
V_GAIN = DT / TAU_M
V_KEEP = 1.0 - V_GAIN
X_KEEP = 1.0 - 1.0 / X_DECAY

J_COLS = slice(0, NEURONS)
V_COLS = slice(NEURONS, 2 * NEURONS)
X_COLS = slice(2 * NEURONS, 3 * NEURONS)
S_COLS = slice(3 * NEURONS, 4 * NEURONS)


def by_tile(dram):
    return dram.rearrange("(p t) c -> p t c", t=TILES)


def k_onto_partitions(nc, banks, ident, block_a, block_b, grouped_words, order):
    turned = banks.tile([P, 2, WORD_HALVES, P], F32, name="turned")
    for i, block in enumerate((block_a, block_b)):
        for u in range(WORD_HALVES):
            nc.tensor.transpose(turned[:, i, u, :], block[:, u * P : (u + 1) * P], ident[:])
    nc.scalar.copy(out=grouped_words, in_=turned[:].rearrange("p i u r -> " + order))


def tile_bspncn_pb_kernel(
    tc, e_gen2, e_disc2, e_gen1, e_disc3, j2, v2, x2, Eg1, Ed2, out
):
    nc = tc.nc
    with ExitStack() as ctx:
        const = ctx.enter_context(tc.tile_pool(name="const", bufs=1))
        inputs = ctx.enter_context(tc.tile_pool(name="inputs", bufs=1))
        head = ctx.enter_context(tc.tile_pool(name="head", bufs=2))
        rests = ctx.enter_context(tc.tile_pool(name="rests", bufs=TILES // 2))
        work = ctx.enter_context(tc.tile_pool(name="work", bufs=3))
        ahead = ctx.enter_context(tc.tile_pool(name="ahead", bufs=4))
        turned_pool = ctx.enter_context(tc.tile_pool(name="turned_pool", bufs=6))
        streams = ctx.enter_context(tc.tile_pool(name="streams", bufs=4))
        results = ctx.enter_context(tc.tile_pool(name="results", bufs=6))
        banks = ctx.enter_context(tc.psum_pool(name="banks", bufs=4))
        sums = ctx.enter_context(tc.psum_pool(name="sums", bufs=4))

        ident = const.tile([P, P], F32, name="ident")
        make_identity(nc, ident[:])
        ident_bf = const.tile([P, P], BF16, name="ident_bf")
        make_identity(nc, ident_bf[:])
        minus_one = const.tile([P, P], BF16, name="minus_one")
        nc.scalar.mul(out=minus_one[:], in_=ident_bf[:], mul=-1.0)
        j_ratio = const.tile([P, P], BF16, name="j_ratio")
        nc.scalar.mul(out=j_ratio[:], in_=ident_bf[:], mul=J_RATIO)

        sources = {
            "e_gen2": e_gen2, "e_disc2": e_disc2, "e_gen1": e_gen1, "e_disc3": e_disc3,
            "j2": j2, "v2": v2, "x2": x2,
        }
        where = {}

        def load(names, first, count):
            for name in names:
                sbuf = inputs.tile([P, count, NEURONS], BF16, name="%s_%d" % (name, first))
                nc.sync.dma_start(out=sbuf[:], in_=by_tile(sources[name])[:, first : first + count, :])
                for t in range(first, first + count):
                    where[(name, t)] = (sbuf, t - first)

        def tiles_of(name, first, count):
            sbuf, i = where[(name, first)]
            return sbuf[:, i : i + count, :]

        w_raw = []

        def load_weights(w):
            raw = const.tile([P, W_BLOCKS, K], BF16, name="w_raw%d" % len(w_raw))
            nc.sync.dma_start(out=raw[:], in_=w.rearrange("(p r) k -> p r k", r=W_BLOCKS))
            w_raw.append(raw)

        own = ("e_gen2", "e_disc2", "j2")
        load(own, 0, 2)
        own = ("j2", "e_gen2", "e_disc2")
        load(own, 2, 4)
        load_weights(Eg1)
        load_weights(Ed2)
        load(("e_gen1", "e_disc3"), 0, 2)
        load(("e_gen1", "e_disc3"), 2, 2)
        load(("v2", "x2"), 0, 4)
        load(("e_gen1", "e_disc3", "v2", "x2"), 4, 4)
        load(own, 6, 2)

        rest = []

        def own_errors(first, chunks):
            j_kept = head.tile([P, 2, NEURONS], F32, name="j_kept")
            own_err = head.tile([P, 2, NEURONS], F32, name="own_err")
            step = 2 // chunks
            for a in range(0, 2, step):
                nc.scalar.mul(out=j_kept[:, a : a + step, :], in_=tiles_of("j2", first + a, step), mul=J_KEEP)
            for a in range(2):
                nc.vector.tensor_tensor(
                    out=own_err[:, a, :], in0=tiles_of("e_gen2", first + a, 1)[:, 0, :],
                    in1=tiles_of("e_disc2", first + a, 1)[:, 0, :], op=ALU.add,
                )
            rest.append(rests.tile([P, 2, NEURONS], F32, name="rest"))
            return j_kept, own_err

        def product_free(t, parts):
            j_kept, own_err = parts
            nc.vector.scalar_tensor_tensor(
                out=rest[t // 2][:, t % 2, :], in0=own_err[:, t % 2, :], scalar=-J_GAIN,
                in1=j_kept[:, t % 2, :], op0=ALU.mult, op1=ALU.add,
            )

        def sum_on_tensor(t):
            acc = sums.tile([P, NEURONS], F32, name="acc")
            terms = ((minus_one, "e_gen2"), (minus_one, "e_disc2"), (j_ratio, "j2"))
            for i, (factor, name) in enumerate(terms):
                nc.tensor.matmul(
                    out=acc[:], lhsT=factor[:], rhs=tiles_of(name, t, 1)[:, 0, :],
                    start=(i == 0), stop=(i == len(terms) - 1),
                )
            return acc

        def product_free_from_sum(t, acc):
            nc.scalar.mul(out=rest[t // 2][:, t % 2, :], in_=acc[:], mul=J_GAIN)

        w_grouped = const.tile([P, 2, NEURONS, PACK], BF16, name="w_grouped", align_bytes=64)
        w_codes = const.tile([P, 2, NEURONS], U32, name="w_codes", align_bytes=64)
        w_scales = const.tile([P, 2, NEURONS], U8, name="w_scales", align_bytes=64)

        def turn_weights(o):
            raw_words = w_raw[o][:].bitcast(F32)
            for r in range(0, W_BLOCKS, 2):
                k_onto_partitions(
                    nc, banks, ident, raw_words[:, r, :], raw_words[:, r + 1, :],
                    w_grouped[:].bitcast(F32)[:, o].rearrange("q (p r) u -> q p r u", r=W_BLOCKS)[:, :, r : r + 2, :],
                    "p r i u",
                )

        def quantise_weights(o):
            nc.vector.quantize_mx(
                out=w_codes[:, o, :].bitcast(FP8X4),
                scales=w_scales[:, o, :],
                in_=w_grouped[:, o].rearrange("p n j -> p (n j)"),
            )

        def turn_streams(t):
            grouped = turned_pool.tile([P, 2, P, PACK], BF16, name="grouped", align_bytes=64)
            k_onto_partitions(
                nc, banks, ident,
                tiles_of("e_gen1", t, 1).bitcast(F32)[:, 0, :],
                tiles_of("e_disc3", t, 1).bitcast(F32)[:, 0, :],
                grouped[:].bitcast(F32),
                "p i r u",
            )
            return grouped

        def quantise_streams(grouped):
            codes = streams.tile([P, 2, P], U32, name="codes", align_bytes=64)
            scales = streams.tile([P, 2, P], U8, name="scales", align_bytes=64)
            nc.vector.quantize_mx(
                out=codes[:].rearrange("p o r -> p (o r)").bitcast(FP8X4),
                scales=scales[:].rearrange("p o r -> p (o r)"),
                in_=grouped[:].rearrange("p o r j -> p (o r j)"),
            )
            return codes, scales

        def keep_potential(t):
            v_kept = ahead.tile([P, NEURONS], F32, name="v_kept")
            nc.scalar.mul(out=v_kept[:], in_=tiles_of("v2", t, 1)[:, 0, :], mul=V_KEEP)
            return v_kept

        def multiply(codes, scales):
            acc = sums.tile([P, NEURONS], F32, name="acc")
            for o in range(2):
                nc.tensor.matmul_mx(
                    out=acc[:],
                    lhsT=codes[:, o, :].bitcast(FP8X4),
                    lhsT_scale=scales[:, o, :],
                    rhs=w_codes[:, o, :].bitcast(FP8X4),
                    rhs_scale=w_scales[:, o, :],
                    start=(o == 0),
                    stop=(o == 1),
                )
            return acc

        res = {}
        v_pre = {}
        turned = {}
        quantised = {}
        fed_back = {}
        v_kept = {}

        def current(t):
            res[t] = results.tile([P, 4 * NEURONS], F32, name="res")
            nc.vector.scalar_tensor_tensor(
                out=res[t][:, J_COLS], in0=fed_back[t][:], scalar=J_GAIN,
                in1=rest[t // 2][:, t % 2, :], op0=ALU.mult, op1=ALU.add,
            )

        def potential(t):
            v_pre[t] = work.tile([P, NEURONS], F32, name="v_pre")
            nc.vector.scalar_tensor_tensor(
                out=v_pre[t][:], in0=res[t][:, J_COLS], scalar=V_GAIN,
                in1=v_kept[t][:], op0=ALU.mult, op1=ALU.add,
            )

        def spikes(t):
            sgn = work.tile([P, NEURONS], F32, name="sgn")
            nc.scalar.activation(out=sgn[:], in_=v_pre[t][:], func=ACT.Sign, bias=-THRESH, scale=1.0)
            nc.scalar.activation(out=res[t][:, S_COLS], in_=sgn[:], func=ACT.Relu)

        def reset(t):
            nc.vector.scalar_tensor_tensor(
                out=res[t][:, V_COLS], in0=v_pre[t][:], scalar=THRESH,
                in1=v_pre[t][:], op0=ALU.is_le, op1=ALU.mult,
            )
            cols = slice(0, 2 * NEURONS)
            nc.sync.dma_start(out=by_tile(out)[:, t, cols], in_=res[t][:, cols])

        def trace(t):
            nc.vector.scalar_tensor_tensor(
                out=res[t][:, X_COLS], in0=tiles_of("x2", t, 1)[:, 0, :], scalar=X_KEEP,
                in1=res[t][:, S_COLS], op0=ALU.mult, op1=ALU.add,
            )
            nc.sync.dma_start(
                out=by_tile(out)[:, t, 2 * NEURONS : 4 * NEURONS], in_=res[t][:, 2 * NEURONS : 4 * NEURONS]
            )

        def keep_trace(t):
            x_kept = const.tile([P, NEURONS], F32, name="x_kept")
            nc.scalar.mul(out=x_kept[:], in_=tiles_of("x2", t, 1)[:, 0, :], mul=X_KEEP)
            return x_kept

        def last_trace(t, x_kept):
            nc.vector.scalar_tensor_tensor(
                out=res[t][:, X_COLS], in0=v_pre[t][:], scalar=THRESH,
                in1=x_kept[:], op0=ALU.is_gt, op1=ALU.add,
            )
            nc.sync.dma_start(
                out=by_tile(out)[:, t, 2 * NEURONS : 4 * NEURONS], in_=res[t][:, 2 * NEURONS : 4 * NEURONS]
            )

        parts = own_errors(0, 1)
        product_free(0, parts)
        product_free(1, parts)
        parts = own_errors(2, 1)
        product_free(2, parts)
        product_free(3, parts)
        parts = own_errors(4, 1)
        turn_weights(0)
        product_free(4, parts)
        product_free(5, parts)
        quantise_weights(0)
        turn_weights(1)
        for t in range(3):
            turned[t] = turn_streams(t)
        quantise_weights(1)
        quantised[0] = quantise_streams(turned[0])
        quantised[1] = quantise_streams(turned[1])
        fed_back[0] = multiply(*quantised[0])
        fed_back[1] = multiply(*quantised[1])
        for t in range(2):
            v_kept[t] = keep_potential(t)
        turned[3] = turn_streams(3)
        current(0)
        quantised[2] = quantise_streams(turned[2])
        potential(0)
        spikes(0)
        v_kept[2] = keep_potential(2)
        rest.append(rests.tile([P, 2, NEURONS], F32, name="rest"))

        for t in range(TILES):
            if t + 2 < TILES:
                fed_back[t + 2] = multiply(*quantised[t + 2])
            if t + 1 < TILES:
                current(t + 1)
            reset(t)
            if t + 1 < TILES:
                potential(t + 1)
                spikes(t + 1)
            if t + 3 < TILES:
                v_kept[t + 3] = keep_potential(t + 3)
            if t + 4 < TILES:
                turned[t + 4] = turn_streams(t + 4)
            if t == 2:
                sums_67 = [sum_on_tensor(6), sum_on_tensor(7)]
            if t == 3:
                product_free_from_sum(6, sums_67[0])
                product_free_from_sum(7, sums_67[1])
            if t + 3 == TILES:
                x_kept = keep_trace(TILES - 1)
            if t + 1 < TILES:
                trace(t)
            else:
                last_trace(t, x_kept)
            if t + 3 < TILES:
                quantised[t + 3] = quantise_streams(turned[t + 3])
